import numpy as np
import ml_dtypes


def mxq(x, axis, fmt="e4m3"):
    dtype, down = {"e4m3": (ml_dtypes.float8_e4m3fn, 7), "e5m2": (ml_dtypes.float8_e5m2, 14)}[fmt]
    v = np.moveaxis(np.asarray(x, np.float32).astype(ml_dtypes.bfloat16).astype(np.float64), axis, -1)
    blocks = v.reshape(v.shape[:-1] + (-1, 32))
    amax = np.abs(blocks).max(-1, keepdims=True)
    byte = np.maximum(np.where(amax > 0, np.frexp(amax)[1] - 1 + 127, 0) - down, 1)
    scale = np.exp2(byte - 127.0)
    codes = (blocks / scale).astype(np.float32).astype(dtype).astype(np.float64)
    return np.moveaxis((codes * scale).reshape(v.shape), -1, axis)


WIDE = False


def mx_kscale(k):
    if not WIDE:
        return np.ones(k)
    levels = np.array([10, -10, 5, -5, 0])
    a = np.random.permutation(np.resize(levels, k // 512 * 4)).reshape(k // 512, 4)
    idx = np.arange(k)
    return np.exp2(a[idx // 512, idx % 128 // 32])


BF16 = ml_dtypes.bfloat16


def bf(x):
    return np.asarray(x, np.float32).astype(BF16)


def f64(x):
    return np.asarray(x).astype(np.float64)


E2M1 = np.array([0.0, 0.5, 1.0, 1.5, 2.0, 3.0, 4.0, 6.0, -0.0, -0.5, -1.0, -1.5, -2.0, -3.0, -4.0, -6.0])


def pack_weight(w, fmt):
    k, n = w.shape
    w = f64(bf(w)).reshape(k // 32, 32, n)
    amax = np.abs(w).max(1)
    if fmt == "e4m3":
        byte = np.frexp(amax)[1] - 1 + 127 - 7
    else:
        mant, ex = np.frexp(amax / 6.0)
        byte = np.where(mant > 0.5, ex, ex - 1) + 127
    byte = np.clip(np.where(amax > 0, byte, 1), 1, 254)
    scaled = (w * np.exp2(127.0 - byte)[:, None, :]).reshape(k, n).astype(np.float32)
    by_word = np.ascontiguousarray(scaled.reshape(k // 512, 128, 4, n).transpose(0, 1, 3, 2))
    if fmt == "e4m3":
        words = by_word.astype(ml_dtypes.float8_e4m3fn).view(np.uint8)
    else:
        c = by_word.astype(ml_dtypes.float4_e2m1fn).view(np.uint8) & 0xF
        words = c[..., 0::2] | (c[..., 1::2] << 4)
    return np.ascontiguousarray(words), np.ascontiguousarray(byte.astype(np.uint8).reshape(k // 512, 16, n))


def unpack_weight(words, scales, fmt):
    g, p, n, _ = words.shape
    if fmt == "e4m3":
        vals = np.ascontiguousarray(words).view(ml_dtypes.float8_e4m3fn).astype(np.float64)
    else:
        nib = np.empty((g, p, n, 4), np.uint8)
        nib[..., 0::2] = words & 0xF
        nib[..., 1::2] = words >> 4
        vals = E2M1[nib]
    vals = vals * np.repeat(np.exp2(scales.astype(np.float64) - 127.0), 8, axis=1)[..., None]
    return vals.transpose(0, 1, 3, 2).reshape(g * 512, n)


N, E, C = 512, 4096, 512
DENSITY = 0.01
FMT = "e4m3"


def setup_inputs():
    s, t = mx_kscale(N), mx_kscale(C)
    member = np.random.uniform(size=(N, E)) < DENSITY
    node_features = bf(np.random.standard_normal((N, C)) / s[:, None] * t[None, :])
    incidence = bf(member * s[:, None])
    words, scales = pack_weight(np.random.standard_normal((C, C)) * np.sqrt(E) / np.sqrt(DENSITY * N * C) / t[:, None], FMT)
    return {"node_features": node_features,
            "incidence": incidence,
            "W1_words": words,
            "W1_scales": scales,
            "b1": bf(np.random.standard_normal(C) * 0.1 * np.sqrt(E)),
            "edge_attention": bf(1.0 + np.random.standard_normal(E))}


def reference(node_features, incidence, W1_words, W1_scales, b1, edge_attention):
    agg = mxq(f64(incidence), 0, "e4m3").T @ mxq(f64(node_features), 0, "e4m3")
    lin = (mxq(agg, 1, "e4m3") @ unpack_weight(W1_words, W1_scales, FMT)) + f64(b1)
    a = f64(edge_attention)
    e = np.exp(a - a.max())
    attn = e / e.sum()
    return lin * attn[:, None]

@@ -1,0 +1,260 @@
+from contextlib import ExitStack
+
+import concourse.mybir as mybir
+from concourse.masks import make_identity
+
+F32 = mybir.dt.float32
+BF16 = mybir.dt.bfloat16
+I32 = mybir.dt.int32
+U32 = mybir.dt.uint32
+U8 = mybir.dt.uint8
+FP8X4 = mybir.dt.float8_e4m3fn_x4
+ALU = mybir.AluOpType
+ACT = mybir.ActivationFunctionType
+AXIS = mybir.AxisListType
+
+P = 128
+PACK = 4
+NODES = 512
+EDGES = 4096
+CHANNELS = 512
+CHUNK = 512
+N_CHUNKS = EDGES // CHUNK
+TILES = CHUNK // P
+QUARTER = P // TILES
+
+FLOPS = 2 * EDGES * NODES * CHANNELS + 2 * EDGES * CHANNELS * CHANNELS
+
+
+def tile_heterogeneoustemporalhypergraphnn_pa_t_kernel(
+    tc, node_features, incidence, W1_words, W1_scales, b1, edge_attention, out
+):
+    nc = tc.nc
+    with ExitStack() as ctx:
+        keep = ctx.enter_context(tc.tile_pool(name="keep", bufs=1))
+        raw = ctx.enter_context(tc.tile_pool(name="raw", bufs=N_CHUNKS))
+        two = ctx.enter_context(tc.tile_pool(name="two", bufs=2))
+        three = ctx.enter_context(tc.tile_pool(name="three", bufs=3))
+        psum_agg = ctx.enter_context(tc.psum_pool(name="psum_agg", bufs=4))
+        psum_lin = ctx.enter_context(tc.psum_pool(name="psum_lin", bufs=4))
+        ctx.enter_context(tc.manual_schedule())
+
+        w_plane = keep.tile([P, CHANNELS], U8, align_bytes=64)
+        nc.vector.memset(w_plane[:].bitcast(I32), 0)
+
+        logits = keep.tile([P, N_CHUNKS, TILES], BF16)
+        with nc.allow_non_contiguous_dma(reason="4,096 logits in runs of 4"):
+            nc.scalar.dma_start(
+                out=logits[:], in_=edge_attention.rearrange("(g q j) -> q g j", q=P, j=TILES)
+            )
+
+        nf_raw = keep.tile([P, PACK, CHANNELS], BF16)
+        nc.sync.dma_start(out=nf_raw[:], in_=node_features.rearrange("(p r) c -> p r c", r=PACK))
+
+        inc_rows = incidence.rearrange("(p r) e -> p r e", r=PACK)
+        inc_raw = []
+
+        def load_incidence(g):
+            chunk_raw = raw.tile([P, PACK, CHUNK], BF16)
+            nc.sync.dma_start(out=chunk_raw[:], in_=inc_rows[:, :, g * CHUNK : (g + 1) * CHUNK])
+            inc_raw.append(chunk_raw)
+
+        load_incidence(0)
+        load_incidence(1)
+
+        w_words = keep.tile([P, CHANNELS * PACK], U8, align_bytes=64)
+        nc.sync.dma_start(
+            out=w_words[:].bitcast(I32), in_=W1_words[0].rearrange("p n t -> p (n t)").bitcast(I32)
+        )
+        for quadrant in range(4):
+            nc.sync.dma_start(
+                out=w_plane[32 * quadrant : 32 * quadrant + 4, :].bitcast(I32),
+                in_=W1_scales[0, 4 * quadrant : 4 * quadrant + 4, :].bitcast(I32),
+            )
+        for g in range(2, N_CHUNKS):
+            load_incidence(g)
+
+        identity = keep.tile([P, P], F32)
+        make_identity(nc, identity[:])
+        ones = keep.tile([P, P], BF16)
+        nc.gpsimd.memset(ones[:], 1.0)
+        b1_row = keep.tile([P, CHANNELS], BF16)
+        nc.gpsimd.memset(b1_row[:], 0.0)
+        nc.scalar.dma_start(out=b1_row[0:1, :], in_=b1.rearrange("(o n) -> o n", o=1))
+
+        def every_partition_sees(column):
+            repeated = two.tile([P, P], F32)
+            nc.vector.tensor_copy(out=repeated[:], in_=column.to_broadcast([P, P]))
+            across = psum_lin.tile([P, P], F32, tag="lin_ps")
+            nc.tensor.transpose(across[:], repeated[:], identity[:])
+            return across
+
+        inc_grouped = {}
+        inc_codes = {}
+        inc_scales = {}
+        agg_grouped = {}
+        agg_codes = {}
+        agg_scales = {}
+        bias_attn = {}
+
+        def regroup_incidence(g):
+            grouped = two.tile([P, CHUNK, PACK], BF16, align_bytes=64, tag="inc_grouped")
+            nc.vector.tensor_copy(
+                out=grouped[:].rearrange("p (c i) r -> p c r i", i=4),
+                in_=inc_raw[g][:].rearrange("p r (c i) -> p c r i", i=4),
+            )
+            inc_grouped[g] = grouped
+
+        def quantise_incidence(g):
+            codes = three.tile([P, CHUNK], U32, align_bytes=64, tag="inc_codes")
+            scales = three.tile([P, CHUNK], U8, align_bytes=64, tag="inc_scales")
+            nc.vector.quantize_mx(
+                out=codes[:].bitcast(FP8X4),
+                scales=scales[:],
+                in_=inc_grouped[g][:].rearrange("p e r -> p (e r)"),
+            )
+            inc_codes[g] = codes
+            inc_scales[g] = scales
+
+        def aggregate(g):
+            grouped = three.tile([P, TILES, P, PACK], BF16, align_bytes=64, tag="agg_grouped")
+            for bank in range(TILES):
+                agg_ps = psum_agg.tile([P, PACK, P], F32)
+                edges = slice(bank * P, (bank + 1) * P)
+                for t in range(PACK):
+                    block = slice(t * P, (t + 1) * P)
+                    nc.tensor.matmul_mx(
+                        out=agg_ps[:, t, :],
+                        lhsT=nf_codes[:, block].bitcast(FP8X4),
+                        lhsT_scale=nf_scales[:, block],
+                        rhs=inc_codes[g][:, edges].bitcast(FP8X4),
+                        rhs_scale=inc_scales[g][:, edges],
+                        start=True,
+                        stop=True,
+                    )
+                nc.scalar.copy(
+                    out=grouped[:, :, bank * QUARTER : (bank + 1) * QUARTER, :],
+                    in_=agg_ps[:].rearrange("p t (q j) -> p j q t", j=TILES),
+                )
+            agg_grouped[g] = grouped
+
+        def quantise_agg(g):
+            codes = two.tile([P, CHUNK], U32, align_bytes=64, tag="agg_codes")
+            scales = two.tile([P, CHUNK], U8, align_bytes=64, tag="agg_scales")
+            nc.vector.quantize_mx(
+                out=codes[:].bitcast(FP8X4),
+                scales=scales[:],
+                in_=agg_grouped[g][:].rearrange("p j q t -> p (j q t)"),
+            )
+            agg_codes[g] = codes
+            agg_scales[g] = scales
+
+        def scale_bias(g):
+            scaled = two.tile([P, TILES, CHANNELS], F32, tag="bias_attn")
+            for j in range(TILES):
+                nc.scalar.activation(
+                    out=scaled[:, j, :], in_=b1_all[:], func=ACT.Copy, scale=attn[:, g, j : j + 1]
+                )
+            bias_attn[g] = scaled
+
+        def project(g):
+            banks = []
+            for j in range(TILES):
+                lin_ps = psum_lin.tile([P, CHANNELS], F32)
+                edges = slice(j * P, (j + 1) * P)
+                nc.tensor.matmul_mx(
+                    out=lin_ps[:],
+                    lhsT=agg_codes[g][:, edges].bitcast(FP8X4),
+                    lhsT_scale=agg_scales[g][:, edges],
+                    rhs=w_words[:].bitcast(FP8X4),
+                    rhs_scale=w_plane[:],
+                    start=True,
+                    stop=True,
+                )
+                banks.append(lin_ps)
+            return banks
+
+        def scale_and_store(g, banks):
+            result = three.tile([P, TILES, CHANNELS], F32)
+            for j in range(TILES):
+                nc.vector.scalar_tensor_tensor(
+                    out=result[:, j, :],
+                    in0=banks[j][:],
+                    scalar=attn[:, g, j : j + 1],
+                    in1=bias_attn[g][:, j, :],
+                    op0=ALU.mult,
+                    op1=ALU.add,
+                )
+            nc.sync.dma_start(
+                out=out[g * CHUNK : (g + 1) * CHUNK, :].rearrange("(q j) n -> q j n", j=TILES),
+                in_=result[:],
+            )
+
+        flat_logits = logits[:].rearrange("q g j -> q (g j)")
+        row_max = keep.tile([P, 1], F32)
+        nc.vector.reduce_max(out=row_max[:], in_=flat_logits, axis=AXIS.X)
+        all_row_max = every_partition_sees(row_max[:])
+
+        b1_ps = psum_lin.tile([P, CHANNELS], F32, tag="lin_ps")
+        nc.tensor.matmul(out=b1_ps[:], lhsT=ones[:], rhs=b1_row[:], start=True, stop=True)
+        b1_all = keep.tile([P, CHANNELS], F32)
+        nc.scalar.copy(out=b1_all[:], in_=b1_ps[:])
+
+        nf_grouped = keep.tile([P, PACK, P, PACK], BF16, align_bytes=64)
+        nc.vector.tensor_copy(
+            out=nf_grouped[:], in_=nf_raw[:].rearrange("p r (q t) -> p t q r", t=PACK)
+        )
+
+        top = keep.tile([P, 1], F32)
+        nc.vector.reduce_max(out=top[:], in_=all_row_max[:], axis=AXIS.X)
+        minus_top = keep.tile([P, 1], F32)
+        nc.vector.tensor_scalar_mul(out=minus_top[:], in0=top[:], scalar1=-1.0)
+        exp_logits = keep.tile([P, N_CHUNKS * TILES], F32)
+        row_sum = keep.tile([P, 1], F32)
+        nc.scalar.activation(
+            out=exp_logits[:],
+            in_=flat_logits,
+            func=ACT.Exp,
+            bias=minus_top[:],
+            scale=1.0,
+            accum_out=row_sum[:],
+        )
+
+        regroup_incidence(0)
+        nf_codes = keep.tile([P, CHANNELS], U32, align_bytes=64)
+        nf_scales = keep.tile([P, CHANNELS], U8, align_bytes=64)
+        nc.vector.quantize_mx(
+            out=nf_codes[:].bitcast(FP8X4),
+            scales=nf_scales[:],
+            in_=nf_grouped[:].rearrange("p t q r -> p (t q r)"),
+        )
+        all_row_sum = every_partition_sees(row_sum[:])
+        quantise_incidence(0)
+        aggregate(0)
+        regroup_incidence(1)
+
+        total = keep.tile([P, 1], F32)
+        nc.vector.reduce_sum(out=total[:], in_=all_row_sum[:], axis=AXIS.X)
+        one_over_total = keep.tile([P, 1], F32)
+        nc.vector.reciprocal(out=one_over_total[:], in_=total[:])
+        attn = keep.tile([P, N_CHUNKS, TILES], F32)
+        nc.vector.tensor_scalar_mul(
+            out=attn[:].rearrange("q g j -> q (g j)"), in0=exp_logits[:], scalar1=one_over_total[:]
+        )
+        scale_bias(0)
+
+        quantise_incidence(1)
+        aggregate(1)
+        regroup_incidence(2)
+
+        for g in range(N_CHUNKS):
+            quantise_agg(g)
+            banks = project(g)
+            if g + 2 < N_CHUNKS:
+                quantise_incidence(g + 2)
+                aggregate(g + 2)
+            if g + 1 < N_CHUNKS:
+                scale_bias(g + 1)
+            if g + 3 < N_CHUNKS:
+                regroup_incidence(g + 3)
+            scale_and_store(g, banks)

@@ -22,6 +22,8 @@ CHUNK = 512
 N_CHUNKS = EDGES // CHUNK
 TILES = CHUNK // P
 QUARTER = P // TILES
+HALF = TILES // 2
+GPSIMD_TILES = 2
 
 FLOPS = 2 * EDGES * NODES * CHANNELS + 2 * EDGES * CHANNELS * CHANNELS
 
@@ -33,6 +35,7 @@ def tile_heterogeneoustemporalhypergraphnn_pa_t_kernel(
     with ExitStack() as ctx:
         keep = ctx.enter_context(tc.tile_pool(name="keep", bufs=1))
         raw = ctx.enter_context(tc.tile_pool(name="raw", bufs=N_CHUNKS))
+        one = ctx.enter_context(tc.tile_pool(name="one", bufs=1))
         two = ctx.enter_context(tc.tile_pool(name="two", bufs=2))
         three = ctx.enter_context(tc.tile_pool(name="three", bufs=3))
         psum_agg = ctx.enter_context(tc.psum_pool(name="psum_agg", bufs=4))
@@ -96,6 +99,7 @@ def tile_heterogeneoustemporalhypergraphnn_pa_t_kernel(
         agg_codes = {}
         agg_scales = {}
         bias_attn = {}
+        lin_banks = {}
 
         def regroup_incidence(g):
             grouped = two.tile([P, CHUNK, PACK], BF16, align_bytes=64, tag="inc_grouped")
@@ -149,13 +153,26 @@ def tile_heterogeneoustemporalhypergraphnn_pa_t_kernel(
             agg_codes[g] = codes
             agg_scales[g] = scales
 
-        def scale_bias(g):
-            scaled = two.tile([P, TILES, CHANNELS], F32, tag="bias_attn")
-            for j in range(TILES):
-                nc.scalar.activation(
-                    out=scaled[:, j, :], in_=b1_all[:], func=ACT.Copy, scale=attn[:, g, j : j + 1]
+        def scale_bias_on_gpsimd(g):
+            for j in range(GPSIMD_TILES):
+                scaled = one.tile([P, CHANNELS], F32, tag="bias_attn_%d" % j)
+                nc.gpsimd.tensor_scalar(
+                    out=scaled[:],
+                    in0=b1_all[:],
+                    scalar1=attn[:, g, j : j + 1],
+                    scalar2=0.0,
+                    op0=ALU.mult,
+                    op1=ALU.add,
                 )
-            bias_attn[g] = scaled
+                bias_attn[(g, j)] = scaled
+
+        def scale_bias_on_scalar(g):
+            for j in range(GPSIMD_TILES, TILES):
+                scaled = two.tile([P, CHANNELS], F32, tag="bias_attn_%d" % j)
+                nc.scalar.activation(
+                    out=scaled[:], in_=b1_all[:], func=ACT.Copy, scale=attn[:, g, j : j + 1]
+                )
+                bias_attn[(g, j)] = scaled
 
         def project(g):
             banks = []
@@ -172,23 +189,39 @@ def tile_heterogeneoustemporalhypergraphnn_pa_t_kernel(
                     stop=True,
                 )
                 banks.append(lin_ps)
-            return banks
+            lin_banks[g] = banks
 
-        def scale_and_store(g, banks):
+        def scale_and_store(g):
             result = three.tile([P, TILES, CHANNELS], F32)
+            rows = out[g * CHUNK : (g + 1) * CHUNK, :].rearrange("(q j) n -> q j n", j=TILES)
             for j in range(TILES):
                 nc.vector.scalar_tensor_tensor(
                     out=result[:, j, :],
-                    in0=banks[j][:],
+                    in0=lin_banks[g][j][:],
                     scalar=attn[:, g, j : j + 1],
-                    in1=bias_attn[g][:, j, :],
+                    in1=bias_attn[(g, j)][:],
                     op0=ALU.mult,
                     op1=ALU.add,
                 )
-            nc.sync.dma_start(
-                out=out[g * CHUNK : (g + 1) * CHUNK, :].rearrange("(q j) n -> q j n", j=TILES),
-                in_=result[:],
-            )
+                if j % HALF == HALF - 1:
+                    pair = slice(j + 1 - HALF, j + 1)
+                    nc.sync.dma_start(out=rows[:, pair, :], in_=result[:, pair, :])
+
+        def pipeline_step(g):
+            if 0 <= g + 3 < N_CHUNKS:
+                quantise_incidence(g + 3)
+                aggregate(g + 3)
+            if 0 <= g + 1 < N_CHUNKS:
+                quantise_agg(g + 1)
+                project(g + 1)
+            if 0 <= g + 4 < N_CHUNKS:
+                regroup_incidence(g + 4)
+            if 0 <= g + 1 < N_CHUNKS:
+                scale_bias_on_scalar(g + 1)
+            if 0 <= g:
+                scale_and_store(g)
+            if 0 <= g + 1 < N_CHUNKS:
+                scale_bias_on_gpsimd(g + 1)
 
         flat_logits = logits[:].rearrange("q g j -> q (g j)")
         row_max = keep.tile([P, 1], F32)
@@ -220,7 +253,8 @@ def tile_heterogeneoustemporalhypergraphnn_pa_t_kernel(
             accum_out=row_sum[:],
         )
 
-        regroup_incidence(0)
+        pipeline_step(-4)
+
         nf_codes = keep.tile([P, CHANNELS], U32, align_bytes=64)
         nf_scales = keep.tile([P, CHANNELS], U8, align_bytes=64)
         nc.vector.quantize_mx(
@@ -229,9 +263,8 @@ def tile_heterogeneoustemporalhypergraphnn_pa_t_kernel(
             in_=nf_grouped[:].rearrange("p t q r -> p (t q r)"),
         )
         all_row_sum = every_partition_sees(row_sum[:])
-        quantise_incidence(0)
-        aggregate(0)
-        regroup_incidence(1)
+
+        pipeline_step(-3)
 
         total = keep.tile([P, 1], F32)
         nc.vector.reduce_sum(out=total[:], in_=all_row_sum[:], axis=AXIS.X)
@@ -241,20 +274,6 @@ def tile_heterogeneoustemporalhypergraphnn_pa_t_kernel(
         nc.vector.tensor_scalar_mul(
             out=attn[:].rearrange("q g j -> q (g j)"), in0=exp_logits[:], scalar1=one_over_total[:]
         )
-        scale_bias(0)
 
-        quantise_incidence(1)
-        aggregate(1)
-        regroup_incidence(2)
-
-        for g in range(N_CHUNKS):
-            quantise_agg(g)
-            banks = project(g)
-            if g + 2 < N_CHUNKS:
-                quantise_incidence(g + 2)
-                aggregate(g + 2)
-            if g + 1 < N_CHUNKS:
-                scale_bias(g + 1)
-            if g + 3 < N_CHUNKS:
-                regroup_incidence(g + 3)
-            scale_and_store(g, banks)
+        for g in range(-2, N_CHUNKS):
+            pipeline_step(g)

@@ -42,14 +42,6 @@ def tile_heterogeneoustemporalhypergraphnn_pa_t_kernel(
         psum_lin = ctx.enter_context(tc.psum_pool(name="psum_lin", bufs=4))
         ctx.enter_context(tc.manual_schedule())
 
-        w_plane = keep.tile([P, CHANNELS], U8, align_bytes=64)
-        nc.vector.memset(w_plane[:].bitcast(I32), 0)
-
-        logits = keep.tile([P, N_CHUNKS, TILES], BF16)
-        with nc.allow_non_contiguous_dma(reason="4,096 logits in runs of 4"):
-            nc.scalar.dma_start(
-                out=logits[:], in_=edge_attention.rearrange("(g q j) -> q g j", q=P, j=TILES)
-            )
 
         nf_raw = keep.tile([P, PACK, CHANNELS], BF16)
         nc.sync.dma_start(out=nf_raw[:], in_=node_features.rearrange("(p r) c -> p r c", r=PACK))
@@ -63,27 +55,36 @@ def tile_heterogeneoustemporalhypergraphnn_pa_t_kernel(
             inc_raw.append(chunk_raw)
 
         load_incidence(0)
-        load_incidence(1)
 
-        w_words = keep.tile([P, CHANNELS * PACK], U8, align_bytes=64)
-        nc.sync.dma_start(
-            out=w_words[:].bitcast(I32), in_=W1_words[0].rearrange("p n t -> p (n t)").bitcast(I32)
-        )
+        logits = keep.tile([P, N_CHUNKS, TILES], BF16)
+        with nc.allow_non_contiguous_dma(reason="4,096 logits in runs of 4"):
+            nc.scalar.dma_start(
+                out=logits[:], in_=edge_attention.rearrange("(g q j) -> q g j", q=P, j=TILES)
+            )
+        b1_row = keep.tile([P, CHANNELS], BF16)
+        nc.gpsimd.memset(b1_row[:], 0.0)
+        nc.scalar.dma_start(out=b1_row[0:1, :], in_=b1.rearrange("(o n) -> o n", o=1))
+
+        w_plane = keep.tile([P, CHANNELS], U8, align_bytes=64)
+        nc.vector.memset(w_plane[:].bitcast(I32), 0)
         for quadrant in range(4):
             nc.sync.dma_start(
                 out=w_plane[32 * quadrant : 32 * quadrant + 4, :].bitcast(I32),
                 in_=W1_scales[0, 4 * quadrant : 4 * quadrant + 4, :].bitcast(I32),
             )
-        for g in range(2, N_CHUNKS):
+        load_incidence(1)
+        load_incidence(2)
+        w_words = keep.tile([P, CHANNELS * PACK], U8, align_bytes=64)
+        nc.sync.dma_start(
+            out=w_words[:].bitcast(I32), in_=W1_words[0].rearrange("p n t -> p (n t)").bitcast(I32)
+        )
+        for g in range(3, N_CHUNKS):
             load_incidence(g)
 
         identity = keep.tile([P, P], F32)
         make_identity(nc, identity[:])
         ones = keep.tile([P, P], BF16)
         nc.gpsimd.memset(ones[:], 1.0)
-        b1_row = keep.tile([P, CHANNELS], BF16)
-        nc.gpsimd.memset(b1_row[:], 0.0)
-        nc.scalar.dma_start(out=b1_row[0:1, :], in_=b1.rearrange("(o n) -> o n", o=1))
 
         def every_partition_sees(column):
             repeated = two.tile([P, P], F32)

@@ -22,7 +22,6 @@ CHUNK = 512
 N_CHUNKS = EDGES // CHUNK
 TILES = CHUNK // P
 QUARTER = P // TILES
-HALF = TILES // 2
 GPSIMD_TILES = 2
 
 FLOPS = 2 * EDGES * NODES * CHANNELS + 2 * EDGES * CHANNELS * CHANNELS
@@ -38,6 +37,7 @@ def tile_heterogeneoustemporalhypergraphnn_pa_t_kernel(
         one = ctx.enter_context(tc.tile_pool(name="one", bufs=1))
         two = ctx.enter_context(tc.tile_pool(name="two", bufs=2))
         three = ctx.enter_context(tc.tile_pool(name="three", bufs=3))
+        results = ctx.enter_context(tc.tile_pool(name="results", bufs=2 * TILES))
         psum_agg = ctx.enter_context(tc.psum_pool(name="psum_agg", bufs=4))
         psum_lin = ctx.enter_context(tc.psum_pool(name="psum_lin", bufs=4))
         ctx.enter_context(tc.manual_schedule())
@@ -193,20 +193,18 @@ def tile_heterogeneoustemporalhypergraphnn_pa_t_kernel(
             lin_banks[g] = banks
 
         def scale_and_store(g):
-            result = three.tile([P, TILES, CHANNELS], F32)
             rows = out[g * CHUNK : (g + 1) * CHUNK, :].rearrange("(q j) n -> q j n", j=TILES)
             for j in range(TILES):
+                result = results.tile([P, CHANNELS], F32)
                 nc.vector.scalar_tensor_tensor(
-                    out=result[:, j, :],
+                    out=result[:],
                     in0=lin_banks[g][j][:],
                     scalar=attn[:, g, j : j + 1],
                     in1=bias_attn[(g, j)][:],
                     op0=ALU.mult,
                     op1=ALU.add,
                 )
-                if j % HALF == HALF - 1:
-                    pair = slice(j + 1 - HALF, j + 1)
-                    nc.sync.dma_start(out=rows[:, pair, :], in_=result[:, pair, :])
+                nc.sync.dma_start(out=rows[:, j, :], in_=result[:])
 
         def pipeline_step(g):
             if 0 <= g + 3 < N_CHUNKS:
@@ -263,9 +261,12 @@ def tile_heterogeneoustemporalhypergraphnn_pa_t_kernel(
             scales=nf_scales[:],
             in_=nf_grouped[:].rearrange("p t q r -> p (t q r)"),
         )
-        all_row_sum = every_partition_sees(row_sum[:])
 
         pipeline_step(-3)
+
+        all_row_sum = every_partition_sees(row_sum[:])
+
+        pipeline_step(-2)
 
         total = keep.tile([P, 1], F32)
         nc.vector.reduce_sum(out=total[:], in_=all_row_sum[:], axis=AXIS.X)
@@ -276,5 +277,5 @@ def tile_heterogeneoustemporalhypergraphnn_pa_t_kernel(
             out=attn[:].rearrange("q g j -> q (g j)"), in0=exp_logits[:], scalar1=one_over_total[:]
         )
 
-        for g in range(-2, N_CHUNKS):
+        for g in range(-1, N_CHUNKS):
             pipeline_step(g)

@@ -23,6 +23,8 @@ N_CHUNKS = EDGES // CHUNK
 TILES = CHUNK // P
 QUARTER = P // TILES
 GPSIMD_TILES = 2
+SCALAR_EDGES = 192
+VECTOR_CHUNKS = (1, 2)
 
 FLOPS = 2 * EDGES * NODES * CHANNELS + 2 * EDGES * CHANNELS * CHANNELS
 
@@ -102,13 +104,24 @@ def tile_heterogeneoustemporalhypergraphnn_pa_t_kernel(
         bias_attn = {}
         lin_banks = {}
 
-        def regroup_incidence(g):
-            grouped = two.tile([P, CHUNK, PACK], BF16, align_bytes=64, tag="inc_grouped")
-            nc.vector.tensor_copy(
-                out=grouped[:].rearrange("p (c i) r -> p c r i", i=4),
-                in_=inc_raw[g][:].rearrange("p r (c i) -> p c r i", i=4),
+        def regroup_incidence(g, copy, edges):
+            if g not in inc_grouped:
+                grouped = two.tile([P, CHUNK, PACK], BF16, align_bytes=64, tag="inc_grouped")
+                inc_grouped[g] = grouped
+            copy(
+                out=inc_grouped[g][:, edges, :].rearrange("p (c i) r -> p c r i", i=4),
+                in_=inc_raw[g][:, :, edges].rearrange("p r (c i) -> p c r i", i=4),
             )
-            inc_grouped[g] = grouped
+
+        def vector_edges(g):
+            return CHUNK if g in VECTOR_CHUNKS else CHUNK - SCALAR_EDGES
+
+        def regroup_on_vector(g):
+            regroup_incidence(g, nc.vector.tensor_copy, slice(0, vector_edges(g)))
+
+        def regroup_on_scalar(g):
+            if vector_edges(g) < CHUNK:
+                regroup_incidence(g, nc.scalar.copy, slice(vector_edges(g), CHUNK))
 
         def quantise_incidence(g):
             codes = three.tile([P, CHUNK], U32, align_bytes=64, tag="inc_codes")
@@ -207,35 +220,42 @@ def tile_heterogeneoustemporalhypergraphnn_pa_t_kernel(
                 nc.sync.dma_start(out=rows[:, j, :], in_=result[:])
 
         def pipeline_step(g):
-            if 0 <= g + 3 < N_CHUNKS:
-                quantise_incidence(g + 3)
-                aggregate(g + 3)
-            if 0 <= g + 1 < N_CHUNKS:
+            if g + 3 < N_CHUNKS:
+                regroup_on_scalar(g + 3)
+            if g + 2 < N_CHUNKS:
+                quantise_incidence(g + 2)
+                aggregate(g + 2)
+            if g + 3 < N_CHUNKS:
+                regroup_on_vector(g + 3)
+            if g + 1 < N_CHUNKS:
                 quantise_agg(g + 1)
                 project(g + 1)
-            if 0 <= g + 4 < N_CHUNKS:
-                regroup_incidence(g + 4)
-            if 0 <= g + 1 < N_CHUNKS:
                 scale_bias_on_scalar(g + 1)
-            if 0 <= g:
-                scale_and_store(g)
-            if 0 <= g + 1 < N_CHUNKS:
+            scale_and_store(g)
+            if g + 1 < N_CHUNKS:
                 scale_bias_on_gpsimd(g + 1)
+
+        nf_grouped = keep.tile([P, PACK, P, PACK], BF16, align_bytes=64)
+        nf_by_block = nf_raw[:].rearrange("p r (q t) -> p t q r", t=PACK)
+        nf_cut = P * 3 // 4
+        nc.vector.tensor_copy(out=nf_grouped[:, :, :nf_cut], in_=nf_by_block[:, :, :nf_cut])
+        nc.scalar.copy(out=nf_grouped[:, :, nf_cut:], in_=nf_by_block[:, :, nf_cut:])
+        regroup_on_scalar(0)
 
         flat_logits = logits[:].rearrange("q g j -> q (g j)")
         row_max = keep.tile([P, 1], F32)
         nc.vector.reduce_max(out=row_max[:], in_=flat_logits, axis=AXIS.X)
         all_row_max = every_partition_sees(row_max[:])
 
-        b1_ps = psum_lin.tile([P, CHANNELS], F32, tag="lin_ps")
-        nc.tensor.matmul(out=b1_ps[:], lhsT=ones[:], rhs=b1_row[:], start=True, stop=True)
-        b1_all = keep.tile([P, CHANNELS], F32)
-        nc.scalar.copy(out=b1_all[:], in_=b1_ps[:])
-
-        nf_grouped = keep.tile([P, PACK, P, PACK], BF16, align_bytes=64)
-        nc.vector.tensor_copy(
-            out=nf_grouped[:], in_=nf_raw[:].rearrange("p r (q t) -> p t q r", t=PACK)
+        nf_codes = keep.tile([P, CHANNELS], U32, align_bytes=64)
+        nf_scales = keep.tile([P, CHANNELS], U8, align_bytes=64)
+        nc.vector.quantize_mx(
+            out=nf_codes[:].bitcast(FP8X4),
+            scales=nf_scales[:],
+            in_=nf_grouped[:].rearrange("p t q r -> p (t q r)"),
         )
+
+        regroup_on_vector(0)
 
         top = keep.tile([P, 1], F32)
         nc.vector.reduce_max(out=top[:], in_=all_row_max[:], axis=AXIS.X)
@@ -252,21 +272,20 @@ def tile_heterogeneoustemporalhypergraphnn_pa_t_kernel(
             accum_out=row_sum[:],
         )
 
-        pipeline_step(-4)
+        quantise_incidence(0)
 
-        nf_codes = keep.tile([P, CHANNELS], U32, align_bytes=64)
-        nf_scales = keep.tile([P, CHANNELS], U8, align_bytes=64)
-        nc.vector.quantize_mx(
-            out=nf_codes[:].bitcast(FP8X4),
-            scales=nf_scales[:],
-            in_=nf_grouped[:].rearrange("p t q r -> p (t q r)"),
-        )
+        b1_ps = psum_lin.tile([P, CHANNELS], F32, tag="lin_ps")
+        nc.tensor.matmul(out=b1_ps[:], lhsT=ones[:], rhs=b1_row[:], start=True, stop=True)
+        b1_all = keep.tile([P, CHANNELS], F32)
+        nc.scalar.copy(out=b1_all[:], in_=b1_ps[:])
 
-        pipeline_step(-3)
-
+        aggregate(0)
         all_row_sum = every_partition_sees(row_sum[:])
 
-        pipeline_step(-2)
+        regroup_on_vector(1)
+        quantise_incidence(1)
+        aggregate(1)
+        regroup_on_vector(2)
 
         total = keep.tile([P, 1], F32)
         nc.vector.reduce_sum(out=total[:], in_=all_row_sum[:], axis=AXIS.X)
@@ -277,5 +296,10 @@ def tile_heterogeneoustemporalhypergraphnn_pa_t_kernel(
             out=attn[:].rearrange("q g j -> q (g j)"), in0=exp_logits[:], scalar1=one_over_total[:]
         )
 
-        for g in range(-1, N_CHUNKS):
+        quantise_agg(0)
+        project(0)
+        scale_bias_on_gpsimd(0)
+        scale_bias_on_scalar(0)
+
+        for g in range(N_CHUNKS):
             pipeline_step(g)

@@ -22,8 +22,8 @@ CHUNK = 512
 N_CHUNKS = EDGES // CHUNK
 TILES = CHUNK // P
 QUARTER = P // TILES
-GPSIMD_TILES = 2
-SCALAR_EDGES = 192
+GPSIMD_TILES = 3
+SCALAR_EDGES = 256
 VECTOR_CHUNKS = (1, 2)
 
 FLOPS = 2 * EDGES * NODES * CHANNELS + 2 * EDGES * CHANNELS * CHANNELS
@@ -169,7 +169,7 @@ def tile_heterogeneoustemporalhypergraphnn_pa_t_kernel(
 
         def scale_bias_on_gpsimd(g):
             for j in range(GPSIMD_TILES):
-                scaled = one.tile([P, CHANNELS], F32, tag="bias_attn_%d" % j)
+                scaled = (one if j == 0 else two).tile([P, CHANNELS], F32, tag="bias_attn_%d" % j)
                 nc.gpsimd.tensor_scalar(
                     out=scaled[:],
                     in0=b1_all[:],

@@ -23,8 +23,10 @@ N_CHUNKS = EDGES // CHUNK
 TILES = CHUNK // P
 QUARTER = P // TILES
 GPSIMD_TILES = 3
+SHARED_CHUNK = N_CHUNKS - 2
+SHARED_TILES = 2
 SCALAR_EDGES = 256
-VECTOR_CHUNKS = (1, 2)
+VECTOR_CHUNKS = (2,)
 
 FLOPS = 2 * EDGES * NODES * CHANNELS + 2 * EDGES * CHANNELS * CHANNELS
 
@@ -103,6 +105,7 @@ def tile_heterogeneoustemporalhypergraphnn_pa_t_kernel(
         agg_scales = {}
         bias_attn = {}
         lin_banks = {}
+        shared_results = {}
 
         def regroup_incidence(g, copy, edges):
             if g not in inc_grouped:
@@ -167,8 +170,11 @@ def tile_heterogeneoustemporalhypergraphnn_pa_t_kernel(
             agg_codes[g] = codes
             agg_scales[g] = scales
 
+        def gpsimd_tiles(g):
+            return 0 if g == N_CHUNKS - 1 else GPSIMD_TILES
+
         def scale_bias_on_gpsimd(g):
-            for j in range(GPSIMD_TILES):
+            for j in range(gpsimd_tiles(g)):
                 scaled = (one if j == 0 else two).tile([P, CHANNELS], F32, tag="bias_attn_%d" % j)
                 nc.gpsimd.tensor_scalar(
                     out=scaled[:],
@@ -181,8 +187,8 @@ def tile_heterogeneoustemporalhypergraphnn_pa_t_kernel(
                 bias_attn[(g, j)] = scaled
 
         def scale_bias_on_scalar(g):
-            for j in range(GPSIMD_TILES, TILES):
-                scaled = two.tile([P, CHANNELS], F32, tag="bias_attn_%d" % j)
+            for j in range(gpsimd_tiles(g), TILES):
+                scaled = two.tile([P, CHANNELS], F32, tag="scalar_bias_attn_%d" % j)
                 nc.scalar.activation(
                     out=scaled[:], in_=b1_all[:], func=ACT.Copy, scale=attn[:, g, j : j + 1]
                 )
@@ -205,9 +211,33 @@ def tile_heterogeneoustemporalhypergraphnn_pa_t_kernel(
                 banks.append(lin_ps)
             lin_banks[g] = banks
 
+        def out_rows(g):
+            return out[g * CHUNK : (g + 1) * CHUNK, :].rearrange("(q j) n -> q j n", j=TILES)
+
+        def shared_tiles(g):
+            return SHARED_TILES if g == SHARED_CHUNK else 0
+
+        def scale_on_scalar(g):
+            for j in range(shared_tiles(g)):
+                scaled_lin = two.tile([P, CHANNELS], F32)
+                nc.scalar.activation(
+                    out=scaled_lin[:],
+                    in_=lin_banks[g][j][:],
+                    func=ACT.Copy,
+                    scale=attn[:, g, j : j + 1],
+                )
+                result = results.tile([P, CHANNELS], F32)
+                nc.gpsimd.tensor_tensor(
+                    out=result[:], in0=scaled_lin[:], in1=bias_attn[(g, j)][:], op=ALU.add
+                )
+                shared_results[(g, j)] = result
+
+        def store_shared(g):
+            for j in range(shared_tiles(g)):
+                nc.scalar.dma_start(out=out_rows(g)[:, j, :], in_=shared_results[(g, j)][:])
+
         def scale_and_store(g):
-            rows = out[g * CHUNK : (g + 1) * CHUNK, :].rearrange("(q j) n -> q j n", j=TILES)
-            for j in range(TILES):
+            for j in range(shared_tiles(g), TILES):
                 result = results.tile([P, CHANNELS], F32)
                 nc.vector.scalar_tensor_tensor(
                     out=result[:],
@@ -217,7 +247,7 @@ def tile_heterogeneoustemporalhypergraphnn_pa_t_kernel(
                     op0=ALU.mult,
                     op1=ALU.add,
                 )
-                nc.sync.dma_start(out=rows[:, j, :], in_=result[:])
+                nc.sync.dma_start(out=out_rows(g)[:, j, :], in_=result[:])
 
         def pipeline_step(g):
             if g + 3 < N_CHUNKS:
@@ -227,11 +257,17 @@ def tile_heterogeneoustemporalhypergraphnn_pa_t_kernel(
                 aggregate(g + 2)
             if g + 3 < N_CHUNKS:
                 regroup_on_vector(g + 3)
+            if g < 2:
+                scale_and_store(g)
             if g + 1 < N_CHUNKS:
                 quantise_agg(g + 1)
                 project(g + 1)
+            scale_on_scalar(g)
+            if g + 1 < N_CHUNKS:
                 scale_bias_on_scalar(g + 1)
-            scale_and_store(g)
+            store_shared(g)
+            if g >= 2:
+                scale_and_store(g)
             if g + 1 < N_CHUNKS:
                 scale_bias_on_gpsimd(g + 1)
 
@@ -276,16 +312,17 @@ def tile_heterogeneoustemporalhypergraphnn_pa_t_kernel(
 
         b1_ps = psum_lin.tile([P, CHANNELS], F32, tag="lin_ps")
         nc.tensor.matmul(out=b1_ps[:], lhsT=ones[:], rhs=b1_row[:], start=True, stop=True)
+
+        regroup_on_scalar(1)
+        aggregate(0)
         b1_all = keep.tile([P, CHANNELS], F32)
         nc.scalar.copy(out=b1_all[:], in_=b1_ps[:])
-
-        aggregate(0)
         all_row_sum = every_partition_sees(row_sum[:])
 
         regroup_on_vector(1)
+        regroup_on_vector(2)
         quantise_incidence(1)
         aggregate(1)
-        regroup_on_vector(2)
 
         total = keep.tile([P, 1], F32)
         nc.vector.reduce_sum(out=total[:], in_=all_row_sum[:], axis=AXIS.X)

@@ -26,7 +26,7 @@ GPSIMD_TILES = 3
 SHARED_CHUNK = N_CHUNKS - 2
 SHARED_TILES = 2
 SCALAR_EDGES = 256
-VECTOR_CHUNKS = (2,)
+HEAD_SCALAR_EDGES = (192, 256, 0)
 
 FLOPS = 2 * EDGES * NODES * CHANNELS + 2 * EDGES * CHANNELS * CHANNELS
 
@@ -38,7 +38,7 @@ def tile_heterogeneoustemporalhypergraphnn_pa_t_kernel(
     with ExitStack() as ctx:
         keep = ctx.enter_context(tc.tile_pool(name="keep", bufs=1))
         raw = ctx.enter_context(tc.tile_pool(name="raw", bufs=N_CHUNKS))
-        one = ctx.enter_context(tc.tile_pool(name="one", bufs=1))
+        rotating = ctx.enter_context(tc.tile_pool(name="rotating", bufs=GPSIMD_TILES + 1))
         two = ctx.enter_context(tc.tile_pool(name="two", bufs=2))
         three = ctx.enter_context(tc.tile_pool(name="three", bufs=3))
         results = ctx.enter_context(tc.tile_pool(name="results", bufs=2 * TILES))
@@ -89,13 +89,8 @@ def tile_heterogeneoustemporalhypergraphnn_pa_t_kernel(
         make_identity(nc, identity[:])
         ones = keep.tile([P, P], BF16)
         nc.gpsimd.memset(ones[:], 1.0)
-
-        def every_partition_sees(column):
-            repeated = two.tile([P, P], F32)
-            nc.vector.tensor_copy(out=repeated[:], in_=column.to_broadcast([P, P]))
-            across = psum_lin.tile([P, P], F32, tag="lin_ps")
-            nc.tensor.transpose(across[:], repeated[:], identity[:])
-            return across
+        ones_f32 = keep.tile([P, P], F32)
+        nc.gpsimd.memset(ones_f32[:], 1.0)
 
         inc_grouped = {}
         inc_codes = {}
@@ -117,7 +112,8 @@ def tile_heterogeneoustemporalhypergraphnn_pa_t_kernel(
             )
 
         def vector_edges(g):
-            return CHUNK if g in VECTOR_CHUNKS else CHUNK - SCALAR_EDGES
+            in_head = g < len(HEAD_SCALAR_EDGES)
+            return CHUNK - (HEAD_SCALAR_EDGES[g] if in_head else SCALAR_EDGES)
 
         def regroup_on_vector(g):
             regroup_incidence(g, nc.vector.tensor_copy, slice(0, vector_edges(g)))
@@ -175,7 +171,7 @@ def tile_heterogeneoustemporalhypergraphnn_pa_t_kernel(
 
         def scale_bias_on_gpsimd(g):
             for j in range(gpsimd_tiles(g)):
-                scaled = (one if j == 0 else two).tile([P, CHANNELS], F32, tag="bias_attn_%d" % j)
+                scaled = rotating.tile([P, CHANNELS], F32, tag="gpsimd_bias_attn")
                 nc.gpsimd.tensor_scalar(
                     out=scaled[:],
                     in0=b1_all[:],
@@ -278,11 +274,6 @@ def tile_heterogeneoustemporalhypergraphnn_pa_t_kernel(
         nc.scalar.copy(out=nf_grouped[:, :, nf_cut:], in_=nf_by_block[:, :, nf_cut:])
         regroup_on_scalar(0)
 
-        flat_logits = logits[:].rearrange("q g j -> q (g j)")
-        row_max = keep.tile([P, 1], F32)
-        nc.vector.reduce_max(out=row_max[:], in_=flat_logits, axis=AXIS.X)
-        all_row_max = every_partition_sees(row_max[:])
-
         nf_codes = keep.tile([P, CHANNELS], U32, align_bytes=64)
         nf_scales = keep.tile([P, CHANNELS], U8, align_bytes=64)
         nc.vector.quantize_mx(
@@ -290,8 +281,22 @@ def tile_heterogeneoustemporalhypergraphnn_pa_t_kernel(
             scales=nf_scales[:],
             in_=nf_grouped[:].rearrange("p t q r -> p (t q r)"),
         )
-
         regroup_on_vector(0)
+
+        flat_logits = logits[:].rearrange("q g j -> q (g j)")
+        row_max = keep.tile([P, 1], F32)
+        nc.vector.reduce_max(out=row_max[:], in_=flat_logits, axis=AXIS.X)
+        all_row_max = psum_lin.tile([P, P], F32, tag="lin_ps")
+        nc.tensor.matmul(
+            out=all_row_max[:],
+            lhsT=row_max[:].to_broadcast([P, P]),
+            rhs=identity[:],
+            start=True,
+            stop=True,
+        )
+
+        quantise_incidence(0)
+        regroup_on_scalar(1)
 
         top = keep.tile([P, 1], F32)
         nc.vector.reduce_max(out=top[:], in_=all_row_max[:], axis=AXIS.X)
@@ -308,29 +313,31 @@ def tile_heterogeneoustemporalhypergraphnn_pa_t_kernel(
             accum_out=row_sum[:],
         )
 
-        quantise_incidence(0)
+        aggregate(0)
+
+        total = psum_lin.tile([P, 1], F32, tag="lin_ps")
+        nc.tensor.matmul(out=total[:], lhsT=ones_f32[:], rhs=row_sum[:], start=True, stop=True)
 
         b1_ps = psum_lin.tile([P, CHANNELS], F32, tag="lin_ps")
         nc.tensor.matmul(out=b1_ps[:], lhsT=ones[:], rhs=b1_row[:], start=True, stop=True)
-
-        regroup_on_scalar(1)
-        aggregate(0)
         b1_all = keep.tile([P, CHANNELS], F32)
         nc.scalar.copy(out=b1_all[:], in_=b1_ps[:])
-        all_row_sum = every_partition_sees(row_sum[:])
 
         regroup_on_vector(1)
         regroup_on_vector(2)
         quantise_incidence(1)
         aggregate(1)
 
-        total = keep.tile([P, 1], F32)
-        nc.vector.reduce_sum(out=total[:], in_=all_row_sum[:], axis=AXIS.X)
         one_over_total = keep.tile([P, 1], F32)
         nc.vector.reciprocal(out=one_over_total[:], in_=total[:])
         attn = keep.tile([P, N_CHUNKS, TILES], F32)
-        nc.vector.tensor_scalar_mul(
-            out=attn[:].rearrange("q g j -> q (g j)"), in0=exp_logits[:], scalar1=one_over_total[:]
+        nc.gpsimd.tensor_scalar(
+            out=attn[:].rearrange("q g j -> q (g j)"),
+            in0=exp_logits[:],
+            scalar1=one_over_total[:],
+            scalar2=0.0,
+            op0=ALU.mult,
+            op1=ALU.add,
         )
 
         quantise_agg(0)

@@ -22,11 +22,13 @@ CHUNK = 512
 N_CHUNKS = EDGES // CHUNK
 TILES = CHUNK // P
 QUARTER = P // TILES
-GPSIMD_TILES = 3
+AGG_BUFFERS = 3
 SHARED_CHUNK = N_CHUNKS - 2
 SHARED_TILES = 2
-SCALAR_EDGES = 256
+SCALAR_EDGES = 320
 HEAD_SCALAR_EDGES = (192, 256, 0)
+
+EARLY_TILES = {0: 2, N_CHUNKS - 2: 1}
 
 FLOPS = 2 * EDGES * NODES * CHANNELS + 2 * EDGES * CHANNELS * CHANNELS
 
@@ -38,7 +40,7 @@ def tile_heterogeneoustemporalhypergraphnn_pa_t_kernel(
     with ExitStack() as ctx:
         keep = ctx.enter_context(tc.tile_pool(name="keep", bufs=1))
         raw = ctx.enter_context(tc.tile_pool(name="raw", bufs=N_CHUNKS))
-        rotating = ctx.enter_context(tc.tile_pool(name="rotating", bufs=GPSIMD_TILES + 1))
+        agg_pool = ctx.enter_context(tc.tile_pool(name="agg_pool", bufs=AGG_BUFFERS))
         two = ctx.enter_context(tc.tile_pool(name="two", bufs=2))
         three = ctx.enter_context(tc.tile_pool(name="three", bufs=3))
         results = ctx.enter_context(tc.tile_pool(name="results", bufs=2 * TILES))
@@ -134,7 +136,7 @@ def tile_heterogeneoustemporalhypergraphnn_pa_t_kernel(
             inc_scales[g] = scales
 
         def aggregate(g):
-            grouped = three.tile([P, TILES, P, PACK], BF16, align_bytes=64, tag="agg_grouped")
+            grouped = agg_pool.tile([P, TILES, P, PACK], BF16, align_bytes=64, tag="agg_grouped")
             for bank in range(TILES):
                 agg_ps = psum_agg.tile([P, PACK, P], F32)
                 edges = slice(bank * P, (bank + 1) * P)
@@ -167,11 +169,14 @@ def tile_heterogeneoustemporalhypergraphnn_pa_t_kernel(
             agg_scales[g] = scales
 
         def gpsimd_tiles(g):
-            return 0 if g == N_CHUNKS - 1 else GPSIMD_TILES
+            return 0 if g == N_CHUNKS - 1 else TILES
 
         def scale_bias_on_gpsimd(g):
             for j in range(gpsimd_tiles(g)):
-                scaled = rotating.tile([P, CHANNELS], F32, tag="gpsimd_bias_attn")
+                if j == 0:
+                    scaled = agg_pool.tile([P, CHANNELS], F32, align_bytes=64, tag="agg_grouped")
+                else:
+                    scaled = two.tile([P, CHANNELS], F32, tag="gpsimd_bias_attn_%d" % j)
                 nc.gpsimd.tensor_scalar(
                     out=scaled[:],
                     in0=b1_all[:],
@@ -232,8 +237,8 @@ def tile_heterogeneoustemporalhypergraphnn_pa_t_kernel(
             for j in range(shared_tiles(g)):
                 nc.scalar.dma_start(out=out_rows(g)[:, j, :], in_=shared_results[(g, j)][:])
 
-        def scale_and_store(g):
-            for j in range(shared_tiles(g), TILES):
+        def scale_and_store(g, tiles):
+            for j in tiles:
                 result = results.tile([P, CHANNELS], F32)
                 nc.vector.scalar_tensor_tensor(
                     out=result[:],
@@ -253,8 +258,9 @@ def tile_heterogeneoustemporalhypergraphnn_pa_t_kernel(
                 aggregate(g + 2)
             if g + 3 < N_CHUNKS:
                 regroup_on_vector(g + 3)
-            if g < 2:
-                scale_and_store(g)
+            first = shared_tiles(g)
+            cut = first + EARLY_TILES.get(g, 0)
+            scale_and_store(g, range(first, cut))
             if g + 1 < N_CHUNKS:
                 quantise_agg(g + 1)
                 project(g + 1)
@@ -262,8 +268,7 @@ def tile_heterogeneoustemporalhypergraphnn_pa_t_kernel(
             if g + 1 < N_CHUNKS:
                 scale_bias_on_scalar(g + 1)
             store_shared(g)
-            if g >= 2:
-                scale_and_store(g)
+            scale_and_store(g, range(cut, TILES))
             if g + 1 < N_CHUNKS:
                 scale_bias_on_gpsimd(g + 1)
 

@@ -22,10 +22,11 @@ CHUNK = 512
 N_CHUNKS = EDGES // CHUNK
 TILES = CHUNK // P
 QUARTER = P // TILES
+GPSIMD_TILES = 3
 AGG_BUFFERS = 3
 SHARED_CHUNK = N_CHUNKS - 2
-SHARED_TILES = 2
-SCALAR_EDGES = 320
+SHARED_TILES = 1
+SCALAR_EDGES = 256
 HEAD_SCALAR_EDGES = (192, 256, 0)
 
 EARLY_TILES = {0: 2, N_CHUNKS - 2: 1}
@@ -169,7 +170,7 @@ def tile_heterogeneoustemporalhypergraphnn_pa_t_kernel(
             agg_scales[g] = scales
 
         def gpsimd_tiles(g):
-            return 0 if g == N_CHUNKS - 1 else TILES
+            return 0 if g == N_CHUNKS - 1 else GPSIMD_TILES
 
         def scale_bias_on_gpsimd(g):
             for j in range(gpsimd_tiles(g)):
@@ -187,8 +188,8 @@ def tile_heterogeneoustemporalhypergraphnn_pa_t_kernel(
                 )
                 bias_attn[(g, j)] = scaled
 
-        def scale_bias_on_scalar(g):
-            for j in range(gpsimd_tiles(g), TILES):
+        def scale_bias_on_scalar(g, tiles):
+            for j in tiles:
                 scaled = two.tile([P, CHANNELS], F32, tag="scalar_bias_attn_%d" % j)
                 nc.scalar.activation(
                     out=scaled[:], in_=b1_all[:], func=ACT.Copy, scale=attn[:, g, j : j + 1]
@@ -264,9 +265,12 @@ def tile_heterogeneoustemporalhypergraphnn_pa_t_kernel(
             if g + 1 < N_CHUNKS:
                 quantise_agg(g + 1)
                 project(g + 1)
+            if g + 1 < N_CHUNKS:
+                middle = gpsimd_tiles(g + 1) + (TILES - gpsimd_tiles(g + 1)) // 2
+                scale_bias_on_scalar(g + 1, range(gpsimd_tiles(g + 1), middle))
             scale_on_scalar(g)
             if g + 1 < N_CHUNKS:
-                scale_bias_on_scalar(g + 1)
+                scale_bias_on_scalar(g + 1, range(middle, TILES))
             store_shared(g)
             scale_and_store(g, range(cut, TILES))
             if g + 1 < N_CHUNKS:
@@ -348,7 +352,7 @@ def tile_heterogeneoustemporalhypergraphnn_pa_t_kernel(
         quantise_agg(0)
         project(0)
         scale_bias_on_gpsimd(0)
-        scale_bias_on_scalar(0)
+        scale_bias_on_scalar(0, range(GPSIMD_TILES, TILES))
 
         for g in range(N_CHUNKS):
             pipeline_step(g)

from contextlib import ExitStack

import concourse.mybir as mybir
from concourse.masks import make_identity

F32 = mybir.dt.float32
BF16 = mybir.dt.bfloat16
I32 = mybir.dt.int32
U32 = mybir.dt.uint32
U8 = mybir.dt.uint8
FP8X4 = mybir.dt.float8_e4m3fn_x4
ALU = mybir.AluOpType
ACT = mybir.ActivationFunctionType
AXIS = mybir.AxisListType

P = 128
PACK = 4
NODES = 512
EDGES = 4096
CHANNELS = 512
CHUNK = 512
N_CHUNKS = EDGES // CHUNK
TILES = CHUNK // P
QUARTER = P // TILES
GPSIMD_TILES = 3
AGG_BUFFERS = 3
SHARED_CHUNK = N_CHUNKS - 2
SHARED_TILES = 1
SCALAR_EDGES = 256
HEAD_SCALAR_EDGES = (192, 256, 0)

EARLY_TILES = {0: 2, N_CHUNKS - 2: 1}

FLOPS = 2 * EDGES * NODES * CHANNELS + 2 * EDGES * CHANNELS * CHANNELS


def tile_heterogeneoustemporalhypergraphnn_pa_t_kernel(
    tc, node_features, incidence, W1_words, W1_scales, b1, edge_attention, out
):
    nc = tc.nc
    with ExitStack() as ctx:
        keep = ctx.enter_context(tc.tile_pool(name="keep", bufs=1))
        raw = ctx.enter_context(tc.tile_pool(name="raw", bufs=N_CHUNKS))
        agg_pool = ctx.enter_context(tc.tile_pool(name="agg_pool", bufs=AGG_BUFFERS))
        two = ctx.enter_context(tc.tile_pool(name="two", bufs=2))
        three = ctx.enter_context(tc.tile_pool(name="three", bufs=3))
        results = ctx.enter_context(tc.tile_pool(name="results", bufs=2 * TILES))
        psum_agg = ctx.enter_context(tc.psum_pool(name="psum_agg", bufs=4))
        psum_lin = ctx.enter_context(tc.psum_pool(name="psum_lin", bufs=4))
        ctx.enter_context(tc.manual_schedule())


        nf_raw = keep.tile([P, PACK, CHANNELS], BF16)
        nc.sync.dma_start(out=nf_raw[:], in_=node_features.rearrange("(p r) c -> p r c", r=PACK))

        inc_rows = incidence.rearrange("(p r) e -> p r e", r=PACK)
        inc_raw = []

        def load_incidence(g):
            chunk_raw = raw.tile([P, PACK, CHUNK], BF16)
            nc.sync.dma_start(out=chunk_raw[:], in_=inc_rows[:, :, g * CHUNK : (g + 1) * CHUNK])
            inc_raw.append(chunk_raw)

        load_incidence(0)

        logits = keep.tile([P, N_CHUNKS, TILES], BF16)
        with nc.allow_non_contiguous_dma(reason="4,096 logits in runs of 4"):
            nc.scalar.dma_start(
                out=logits[:], in_=edge_attention.rearrange("(g q j) -> q g j", q=P, j=TILES)
            )
        b1_row = keep.tile([P, CHANNELS], BF16)
        nc.gpsimd.memset(b1_row[:], 0.0)
        nc.scalar.dma_start(out=b1_row[0:1, :], in_=b1.rearrange("(o n) -> o n", o=1))

        w_plane = keep.tile([P, CHANNELS], U8, align_bytes=64)
        nc.vector.memset(w_plane[:].bitcast(I32), 0)
        for quadrant in range(4):
            nc.sync.dma_start(
                out=w_plane[32 * quadrant : 32 * quadrant + 4, :].bitcast(I32),
                in_=W1_scales[0, 4 * quadrant : 4 * quadrant + 4, :].bitcast(I32),
            )
        load_incidence(1)
        load_incidence(2)
        w_words = keep.tile([P, CHANNELS * PACK], U8, align_bytes=64)
        nc.sync.dma_start(
            out=w_words[:].bitcast(I32), in_=W1_words[0].rearrange("p n t -> p (n t)").bitcast(I32)
        )
        for g in range(3, N_CHUNKS):
            load_incidence(g)

        identity = keep.tile([P, P], F32)
        make_identity(nc, identity[:])
        ones = keep.tile([P, P], BF16)
        nc.gpsimd.memset(ones[:], 1.0)
        ones_f32 = keep.tile([P, P], F32)
        nc.gpsimd.memset(ones_f32[:], 1.0)

        inc_grouped = {}
        inc_codes = {}
        inc_scales = {}
        agg_grouped = {}
        agg_codes = {}
        agg_scales = {}
        bias_attn = {}
        lin_banks = {}
        shared_results = {}

        def regroup_incidence(g, copy, edges):
            if g not in inc_grouped:
                grouped = two.tile([P, CHUNK, PACK], BF16, align_bytes=64, tag="inc_grouped")
                inc_grouped[g] = grouped
            copy(
                out=inc_grouped[g][:, edges, :].rearrange("p (c i) r -> p c r i", i=4),
                in_=inc_raw[g][:, :, edges].rearrange("p r (c i) -> p c r i", i=4),
            )

        def vector_edges(g):
            in_head = g < len(HEAD_SCALAR_EDGES)
            return CHUNK - (HEAD_SCALAR_EDGES[g] if in_head else SCALAR_EDGES)

        def regroup_on_vector(g):
            regroup_incidence(g, nc.vector.tensor_copy, slice(0, vector_edges(g)))

        def regroup_on_scalar(g):
            if vector_edges(g) < CHUNK:
                regroup_incidence(g, nc.scalar.copy, slice(vector_edges(g), CHUNK))

        def quantise_incidence(g):
            codes = three.tile([P, CHUNK], U32, align_bytes=64, tag="inc_codes")
            scales = three.tile([P, CHUNK], U8, align_bytes=64, tag="inc_scales")
            nc.vector.quantize_mx(
                out=codes[:].bitcast(FP8X4),
                scales=scales[:],
                in_=inc_grouped[g][:].rearrange("p e r -> p (e r)"),
            )
            inc_codes[g] = codes
            inc_scales[g] = scales

        def aggregate(g):
            grouped = agg_pool.tile([P, TILES, P, PACK], BF16, align_bytes=64, tag="agg_grouped")
            for bank in range(TILES):
                agg_ps = psum_agg.tile([P, PACK, P], F32)
                edges = slice(bank * P, (bank + 1) * P)
                for t in range(PACK):
                    block = slice(t * P, (t + 1) * P)
                    nc.tensor.matmul_mx(
                        out=agg_ps[:, t, :],
                        lhsT=nf_codes[:, block].bitcast(FP8X4),
                        lhsT_scale=nf_scales[:, block],
                        rhs=inc_codes[g][:, edges].bitcast(FP8X4),
                        rhs_scale=inc_scales[g][:, edges],
                        start=True,
                        stop=True,
                    )
                nc.scalar.copy(
                    out=grouped[:, :, bank * QUARTER : (bank + 1) * QUARTER, :],
                    in_=agg_ps[:].rearrange("p t (q j) -> p j q t", j=TILES),
                )
            agg_grouped[g] = grouped

        def quantise_agg(g):
            codes = two.tile([P, CHUNK], U32, align_bytes=64, tag="agg_codes")
            scales = two.tile([P, CHUNK], U8, align_bytes=64, tag="agg_scales")
            nc.vector.quantize_mx(
                out=codes[:].bitcast(FP8X4),
                scales=scales[:],
                in_=agg_grouped[g][:].rearrange("p j q t -> p (j q t)"),
            )
            agg_codes[g] = codes
            agg_scales[g] = scales

        def gpsimd_tiles(g):
            return 0 if g == N_CHUNKS - 1 else GPSIMD_TILES

        def scale_bias_on_gpsimd(g):
            for j in range(gpsimd_tiles(g)):
                if j == 0:
                    scaled = agg_pool.tile([P, CHANNELS], F32, align_bytes=64, tag="agg_grouped")
                else:
                    scaled = two.tile([P, CHANNELS], F32, tag="gpsimd_bias_attn_%d" % j)
                nc.gpsimd.tensor_scalar(
                    out=scaled[:],
                    in0=b1_all[:],
                    scalar1=attn[:, g, j : j + 1],
                    scalar2=0.0,
                    op0=ALU.mult,
                    op1=ALU.add,
                )
                bias_attn[(g, j)] = scaled

        def scale_bias_on_scalar(g, tiles):
            for j in tiles:
                scaled = two.tile([P, CHANNELS], F32, tag="scalar_bias_attn_%d" % j)
                nc.scalar.activation(
                    out=scaled[:], in_=b1_all[:], func=ACT.Copy, scale=attn[:, g, j : j + 1]
                )
                bias_attn[(g, j)] = scaled

        def project(g):
            banks = []
            for j in range(TILES):
                lin_ps = psum_lin.tile([P, CHANNELS], F32)
                edges = slice(j * P, (j + 1) * P)
                nc.tensor.matmul_mx(
                    out=lin_ps[:],
                    lhsT=agg_codes[g][:, edges].bitcast(FP8X4),
                    lhsT_scale=agg_scales[g][:, edges],
                    rhs=w_words[:].bitcast(FP8X4),
                    rhs_scale=w_plane[:],
                    start=True,
                    stop=True,
                )
                banks.append(lin_ps)
            lin_banks[g] = banks

        def out_rows(g):
            return out[g * CHUNK : (g + 1) * CHUNK, :].rearrange("(q j) n -> q j n", j=TILES)

        def shared_tiles(g):
            return SHARED_TILES if g == SHARED_CHUNK else 0

        def scale_on_scalar(g):
            for j in range(shared_tiles(g)):
                scaled_lin = two.tile([P, CHANNELS], F32)
                nc.scalar.activation(
                    out=scaled_lin[:],
                    in_=lin_banks[g][j][:],
                    func=ACT.Copy,
                    scale=attn[:, g, j : j + 1],
                )
                result = results.tile([P, CHANNELS], F32)
                nc.gpsimd.tensor_tensor(
                    out=result[:], in0=scaled_lin[:], in1=bias_attn[(g, j)][:], op=ALU.add
                )
                shared_results[(g, j)] = result

        def store_shared(g):
            for j in range(shared_tiles(g)):
                nc.scalar.dma_start(out=out_rows(g)[:, j, :], in_=shared_results[(g, j)][:])

        def scale_and_store(g, tiles):
            for j in tiles:
                result = results.tile([P, CHANNELS], F32)
                nc.vector.scalar_tensor_tensor(
                    out=result[:],
                    in0=lin_banks[g][j][:],
                    scalar=attn[:, g, j : j + 1],
                    in1=bias_attn[(g, j)][:],
                    op0=ALU.mult,
                    op1=ALU.add,
                )
                nc.sync.dma_start(out=out_rows(g)[:, j, :], in_=result[:])

        def pipeline_step(g):
            if g + 3 < N_CHUNKS:
                regroup_on_scalar(g + 3)
            if g + 2 < N_CHUNKS:
                quantise_incidence(g + 2)
                aggregate(g + 2)
            if g + 3 < N_CHUNKS:
                regroup_on_vector(g + 3)
            first = shared_tiles(g)
            cut = first + EARLY_TILES.get(g, 0)
            scale_and_store(g, range(first, cut))
            if g + 1 < N_CHUNKS:
                quantise_agg(g + 1)
                project(g + 1)
            if g + 1 < N_CHUNKS:
                middle = gpsimd_tiles(g + 1) + (TILES - gpsimd_tiles(g + 1)) // 2
                scale_bias_on_scalar(g + 1, range(gpsimd_tiles(g + 1), middle))
            scale_on_scalar(g)
            if g + 1 < N_CHUNKS:
                scale_bias_on_scalar(g + 1, range(middle, TILES))
            store_shared(g)
            scale_and_store(g, range(cut, TILES))
            if g + 1 < N_CHUNKS:
                scale_bias_on_gpsimd(g + 1)

        nf_grouped = keep.tile([P, PACK, P, PACK], BF16, align_bytes=64)
        nf_by_block = nf_raw[:].rearrange("p r (q t) -> p t q r", t=PACK)
        nf_cut = P * 3 // 4
        nc.vector.tensor_copy(out=nf_grouped[:, :, :nf_cut], in_=nf_by_block[:, :, :nf_cut])
        nc.scalar.copy(out=nf_grouped[:, :, nf_cut:], in_=nf_by_block[:, :, nf_cut:])
        regroup_on_scalar(0)

        nf_codes = keep.tile([P, CHANNELS], U32, align_bytes=64)
        nf_scales = keep.tile([P, CHANNELS], U8, align_bytes=64)
        nc.vector.quantize_mx(
            out=nf_codes[:].bitcast(FP8X4),
            scales=nf_scales[:],
            in_=nf_grouped[:].rearrange("p t q r -> p (t q r)"),
        )
        regroup_on_vector(0)

        flat_logits = logits[:].rearrange("q g j -> q (g j)")
        row_max = keep.tile([P, 1], F32)
        nc.vector.reduce_max(out=row_max[:], in_=flat_logits, axis=AXIS.X)
        all_row_max = psum_lin.tile([P, P], F32, tag="lin_ps")
        nc.tensor.matmul(
            out=all_row_max[:],
            lhsT=row_max[:].to_broadcast([P, P]),
            rhs=identity[:],
            start=True,
            stop=True,
        )

        quantise_incidence(0)
        regroup_on_scalar(1)

        top = keep.tile([P, 1], F32)
        nc.vector.reduce_max(out=top[:], in_=all_row_max[:], axis=AXIS.X)
        minus_top = keep.tile([P, 1], F32)
        nc.vector.tensor_scalar_mul(out=minus_top[:], in0=top[:], scalar1=-1.0)
        exp_logits = keep.tile([P, N_CHUNKS * TILES], F32)
        row_sum = keep.tile([P, 1], F32)
        nc.scalar.activation(
            out=exp_logits[:],
            in_=flat_logits,
            func=ACT.Exp,
            bias=minus_top[:],
            scale=1.0,
            accum_out=row_sum[:],
        )

        aggregate(0)

        total = psum_lin.tile([P, 1], F32, tag="lin_ps")
        nc.tensor.matmul(out=total[:], lhsT=ones_f32[:], rhs=row_sum[:], start=True, stop=True)

        b1_ps = psum_lin.tile([P, CHANNELS], F32, tag="lin_ps")
        nc.tensor.matmul(out=b1_ps[:], lhsT=ones[:], rhs=b1_row[:], start=True, stop=True)
        b1_all = keep.tile([P, CHANNELS], F32)
        nc.scalar.copy(out=b1_all[:], in_=b1_ps[:])

        regroup_on_vector(1)
        regroup_on_vector(2)
        quantise_incidence(1)
        aggregate(1)

        one_over_total = keep.tile([P, 1], F32)
        nc.vector.reciprocal(out=one_over_total[:], in_=total[:])
        attn = keep.tile([P, N_CHUNKS, TILES], F32)
        nc.gpsimd.tensor_scalar(
            out=attn[:].rearrange("q g j -> q (g j)"),
            in0=exp_logits[:],
            scalar1=one_over_total[:],
            scalar2=0.0,
            op0=ALU.mult,
            op1=ALU.add,
        )

        quantise_agg(0)
        project(0)
        scale_bias_on_gpsimd(0)
        scale_bias_on_scalar(0, range(GPSIMD_TILES, TILES))

        for g in range(N_CHUNKS):
            pipeline_step(g)
